import numpy as np
import ml_dtypes


def mxq(x, axis, fmt="e4m3"):
    dtype, down = {"e4m3": (ml_dtypes.float8_e4m3fn, 7), "e5m2": (ml_dtypes.float8_e5m2, 14)}[fmt]
    v = np.moveaxis(np.asarray(x, np.float32).astype(ml_dtypes.bfloat16).astype(np.float64), axis, -1)
    blocks = v.reshape(v.shape[:-1] + (-1, 32))
    amax = np.abs(blocks).max(-1, keepdims=True)
    byte = np.maximum(np.where(amax > 0, np.frexp(amax)[1] - 1 + 127, 0) - down, 1)
    scale = np.exp2(byte - 127.0)
    codes = (blocks / scale).astype(np.float32).astype(dtype).astype(np.float64)
    return np.moveaxis((codes * scale).reshape(v.shape), -1, axis)


WIDE = False


def mx_kscale(k):
    if not WIDE:
        return np.ones(k)
    levels = np.array([18, -18])
    if k % 512:
        return np.exp2(np.random.permutation(np.resize(levels, k // 32))).repeat(32)
    a = np.empty((k // 512, 16))
    for p in range(k // 512):
        a[p, :8] = np.random.permutation(np.resize(levels, 8))
        for g in range(8):
            far = levels[np.abs(levels - a[p, g]) >= 10]
            a[p, g + 8] = far[np.random.randint(len(far))]
    return np.exp2(a.ravel()).repeat(32)


BF16 = ml_dtypes.bfloat16


def bf(x):
    return np.asarray(x, np.float32).astype(BF16)


def f64(x):
    return np.asarray(x).astype(np.float64)


B, T, U, D_ENC, D_PRED, D_JOINT, VOCAB = 4, 128, 8, 512, 512, 512, 1024
LOGIT_CLAMP = 15.0


def setup_inputs():
    s = mx_kscale(B * T).reshape(B, T, 1)
    u = mx_kscale(VOCAB)
    v = mx_kscale(D_JOINT)
    enc0 = bf(np.random.standard_normal((B, T, D_ENC)))
    pred0 = bf(np.random.standard_normal((B, U, D_PRED)))
    W_enc0 = bf(np.random.standard_normal((D_ENC, D_JOINT)) * 0.7 / np.sqrt(D_ENC))
    b_enc = bf(np.random.standard_normal(D_JOINT) * 0.2)
    W_pred = bf(np.random.standard_normal((D_PRED, D_JOINT)) * 0.7 / np.sqrt(D_PRED))
    b_pred = bf(np.random.standard_normal(D_JOINT) * 0.2)
    W_out0 = bf(np.random.standard_normal((D_JOINT, VOCAB)) * 8.0 / np.sqrt(D_JOINT))
    b_out = bf(np.random.standard_normal(VOCAB) * 0.5)
    g = bf(0.25 * np.random.standard_normal((B, T, U, VOCAB)) * np.exp2(np.random.randint(-6, 1, (B, T, 1, 1))) / s[:, :, :, None] * u)
    enc = f64(enc0) @ f64(W_enc0) + f64(b_enc)
    pred = f64(pred0) @ f64(W_pred) + f64(b_pred)
    joint = np.tanh(enc[:, :, None, :] + pred[:, None, :, :])
    logits = joint @ f64(W_out0) + f64(b_out)
    return {"encoder_out": bf(f64(enc0) * s),
            "predictor_out": pred0,
            "W_enc": bf(f64(W_enc0) / v),
            "b_enc": b_enc,
            "W_pred": W_pred,
            "b_pred": b_pred,
            "W_out": bf(f64(W_out0) * v[:, None] / u),
            "b_out": b_out,
            "joint": np.asarray(joint, np.float32),
            "logits": np.asarray(logits, np.float32),
            "grad_out": g}


def reference(encoder_out, predictor_out, W_enc, b_enc, W_pred, b_pred, W_out, b_out, joint, logits, grad_out):
    jf = f64(joint)
    dz2 = np.where(np.abs(f64(logits)) <= LOGIT_CLAMP, f64(grad_out), 0.0).reshape(B * T * U, VOCAB)
    dh = mxq(dz2, 1, "e5m2") @ mxq(f64(W_out), 1, "e4m3").T
    dsum = dh.reshape(B, T, U, D_JOINT) * (1.0 - jf * jf)
    denc = dsum.sum(axis=2).reshape(B * T, D_JOINT)
    x = f64(encoder_out).reshape(B * T, D_ENC)
    dx = mxq(denc, 1, "e5m2") @ mxq(f64(W_enc), 1, "e4m3").T
    dw = mxq(x, 0, "e4m3").T @ mxq(denc, 0, "e5m2")
    return dx.reshape(B, T, D_ENC), dw

@@ -1,0 +1,467 @@
+from contextlib import ExitStack
+
+import concourse.mybir as mybir
+from concourse.masks import make_identity
+
+B, T, U, D_ENC, D_JOINT, VOCAB = 4, 128, 8, 512, 512, 1024
+FRAMES = B * T
+FLOPS = 2 * FRAMES * U * VOCAB * D_JOINT + 2 * 2 * FRAMES * D_JOINT * D_ENC
+BYTES = (
+    FRAMES * U * (VOCAB * 4 + VOCAB * 2 + D_JOINT * 4)
+    + 2 * (FRAMES * D_ENC + D_ENC * D_JOINT + D_JOINT * VOCAB)
+    + 4 * (FRAMES * D_ENC + D_ENC * D_JOINT)
+)
+
+F32 = mybir.dt.float32
+BF16 = mybir.dt.bfloat16
+U32 = mybir.dt.uint32
+U8 = mybir.dt.uint8
+E4M3 = mybir.dt.float8_e4m3fn_x4
+E5M2 = mybir.dt.float8_e5m2_x4
+ACT = mybir.ActivationFunctionType
+ALU = mybir.AluOpType
+
+P = 128
+PACK = 4
+BANK = 512
+TILES = PACK * U
+PASSES = VOCAB // (P * PACK)
+ABS_SCALE = 19.0
+ABS_LIMIT = 15.0 * ABS_SCALE
+
+HEAD_SINGLES = 2
+TAIL_SINGLES = 4
+LAG = 0
+STEPS = (
+    [(a, 1) for a in range(HEAD_SINGLES)]
+    + [(a, 2) for a in range(HEAD_SINGLES, TILES - TAIL_SINGLES, 2)]
+    + [(a, 1) for a in range(TILES - TAIL_SINGLES, TILES)]
+)
+STEP_OF = {first + a: i for i, (first, count) in enumerate(STEPS) for a in range(count)}
+READER = {"logits": 0, "grad": 1, "joint": 2 + LAG}
+GQ = -0.5
+JQ = 2.5
+QUEUE = {"logits": 0, "grad": GQ, "joint": JQ + LAG}
+VEC_FROM = 2
+VEC_TO = 28
+WIDE = 4
+LWIDE = 2
+NARROW = 4
+PIECES = {
+    "logits": [s for s in STEPS if s[0] < NARROW] + [(a, LWIDE) for a in range(NARROW, TILES - WIDE, LWIDE)] + [s for s in STEPS if s[0] >= TILES - WIDE],
+    "grad": [(0, 2), (2, 2)] + [(a, WIDE) for a in range(WIDE, TILES - WIDE, WIDE)] + [s for s in STEPS if s[0] >= TILES - WIDE],
+    "joint": [(a, WIDE) for a in range(0, TILES - WIDE, WIDE)] + [s for s in STEPS if s[0] >= TILES - WIDE],
+}
+W_OUT_AT = 1
+W_ENC_AT = 3
+LOADS = [
+    entry[2:]
+    for entry in sorted(
+        [(max(0, STEP_OF[first] + QUEUE[kind]), n, kind, first, count) for n, kind in enumerate(PIECES) for first, count in PIECES[kind]]
+        + [(W_OUT_AT - 1, 3, "w_out", 0, 0), (W_ENC_AT, 3, "w_enc", 0, 0), (len(STEPS) + 3 + LAG, 3, "x", 0, 0)]
+    )
+]
+LOAD_BUFS = {"wide": 3, "single": 4}
+
+
+def tile_jointnetwork_v_kernel(
+    tc, encoder_out, predictor_out, W_enc, b_enc, W_pred, b_pred, W_out, b_out, joint, logits, grad_out, out_0, out_1
+):
+    nc = tc.nc
+
+    def by_frame(x):
+        return x.rearrange("b f u w -> (b f) (u w)").rearrange("(p t) w -> p t w", t=PACK)
+
+    streams = {
+        "logits": (by_frame(logits), VOCAB, F32),
+        "grad": (by_frame(grad_out), VOCAB, BF16),
+        "joint": (by_frame(joint), D_JOINT, F32),
+    }
+    out_0_rows = out_0.rearrange("b f d -> (b f) d").rearrange("(p t) d -> p t d", t=PACK)
+
+    with ExitStack() as ctx:
+        keep = ctx.enter_context(tc.tile_pool(name="keep", bufs=1))
+        stream = ctx.enter_context(tc.tile_pool(name="stream", bufs=1))
+        work = ctx.enter_context(tc.tile_pool(name="work", bufs=2))
+        psum = ctx.enter_context(tc.psum_pool(name="psum", bufs=1))
+        ctx.enter_context(tc.manual_schedule())
+
+        def bank(role):
+            return psum.tile([P, BANK], F32, name="bank_" + role, tag=role)
+
+        def kept(name, width, dtype):
+            return keep.tile([P, width], dtype, name=name, tag=name, align_bytes=64)
+
+        def working(name, width, dtype, bufs=2):
+            return work.tile([P, width], dtype, name=name, tag=name, bufs=bufs, align_bytes=64)
+
+        def copy_on(engine, out, in_):
+            if engine == "scalar":
+                nc.scalar.copy(out=out, in_=in_)
+            else:
+                nc.vector.tensor_copy(out=out, in_=in_)
+
+        loaded = {}
+        held = {}
+
+        def landing(kind, size, width, dtype):
+            name = kind + "_" + size
+            return stream.tile([P, width], dtype, name=name, tag=name, bufs=LOAD_BUFS[size], align_bytes=64)
+
+        def size_of(count):
+            return "single" if count == 1 else "wide"
+
+        w_out_raw = landing("joint", "wide", PACK * VOCAB, BF16)
+        w_out_halves = landing("joint", "wide", PACK * VOCAB, BF16)
+        w_enc_raw = kept("w_enc_raw", PACK * D_JOINT, BF16)
+        x_raw = kept("x_raw", PACK * D_ENC, BF16)
+
+        def load(kind, first, count):
+            if kind == "w_out":
+                nc.sync.dma_start(out=w_out_raw[:], in_=W_out.rearrange("(p s) v -> p (s v)", s=PACK))
+            elif kind == "w_enc":
+                nc.sync.dma_start(out=w_enc_raw[:], in_=W_enc.rearrange("(p s) j -> p (s j)", s=PACK))
+            elif kind == "x":
+                rows = encoder_out.rearrange("b f d -> (b f) d")
+                nc.sync.dma_start(out=x_raw[:], in_=rows.rearrange("(p t) d -> p (t d)", t=PACK))
+            else:
+                source, width, dtype = streams[kind]
+                dst = landing(kind, size_of(count), count * width, dtype)
+                t, u = divmod(first, U)
+                nc.sync.dma_start(out=dst[:], in_=source[:, t, u * width : (u + count) * width])
+                for a in range(count):
+                    loaded[kind, first + a] = (dst, a)
+
+        def streamed(kind, first, count):
+            dst, a = loaded[kind, first]
+            width = streams[kind][1]
+            return dst[:, a * width : (a + count) * width]
+
+        ident_f32 = kept("ident_f32", P, F32)
+        ident_bf16 = kept("ident_bf16", P, BF16)
+        zeros = kept("zeros", BANK, BF16)
+
+        w_out_codes = kept("w_out_codes", PASSES * D_JOINT, U32)
+        w_out_scales = kept("w_out_scales", PASSES * D_JOINT, U8)
+
+        def sort_w_out():
+            halves = w_out_halves
+            nc.vector.tensor_copy(
+                out=halves[:].bitcast(F32).rearrange("p (h b i) -> p b h i", h=2, i=8),
+                in_=w_out_raw[:].bitcast(F32).rearrange("p (b h i) -> p b h i", h=2, i=8),
+            )
+            words = halves[:].bitcast(F32).rearrange("p (h s g q) -> p h s g q", h=2, s=PACK, g=PASSES)
+            for g in range(PASSES):
+                for r in range(2):
+                    turned = bank("dh%d" % (2 * g + r))
+                    for x in range(4):
+                        s, h = 2 * r + x // 2, x % 2
+                        nc.tensor.transpose(turned[:, x * P : (x + 1) * P], words[:, h, s, g, :], ident_f32[:])
+                    held["w_out", g, r] = turned
+
+        def group_w_out():
+            for g in range(PASSES):
+                grouped = kept("w_out_grouped_%d" % g, PACK * D_JOINT, BF16)
+                held["w_out", g] = grouped
+                dst = grouped[:].bitcast(F32).rearrange("p (c b w r x) -> p r b c w x", c=PACK, w=2, r=2, x=4)
+                for r in range(2):
+                    src = held["w_out", g, r][:].rearrange("p (x b c w) -> p b c w x", x=4, c=PACK, w=2)
+                    copy_on(("scalar", "vector")[g], dst[:, r], src)
+
+        def quantize_w_out():
+            for g in range(PASSES):
+                cols = slice(g * D_JOINT, (g + 1) * D_JOINT)
+                nc.vector.quantize_mx(
+                    out=w_out_codes[:, cols].bitcast(E4M3), scales=w_out_scales[:, cols], in_=held["w_out", g][:]
+                )
+
+        w_enc_sorted = kept("w_enc_sorted", PACK * D_JOINT, BF16)
+        w_enc_grouped = kept("w_enc_grouped", PACK * D_ENC, BF16)
+        w_enc_codes = kept("w_enc_codes", D_ENC, U32)
+        w_enc_scales = kept("w_enc_scales", D_ENC, U8)
+
+        def sort_w_enc():
+            nc.vector.tensor_copy(
+                out=w_enc_sorted[:].bitcast(F32).rearrange("p (c b i) -> p b c i", c=PACK, i=4),
+                in_=w_enc_raw[:].bitcast(F32).rearrange("p (b c i) -> p b c i", c=PACK, i=4),
+            )
+
+        def turn_w_enc(r):
+            rows = w_enc_sorted[:].rearrange("p (c s q) -> p c s q", c=PACK, s=PACK)
+            turned = bank("sum1")
+            view = turned[:].bitcast(BF16).rearrange("p (s c d) -> p s c d", s=2, c=PACK)
+            for s in range(2):
+                for c in range(PACK):
+                    nc.tensor.transpose(view[:, s, c, :], rows[:, c, 2 * r + s, :], ident_bf16[:])
+            half = PACK * D_ENC // 2
+            nc.scalar.copy(
+                out=w_enc_grouped[:, r * half : (r + 1) * half].rearrange("p (s d c) -> p s d c", s=2, c=PACK),
+                in_=view.rearrange("p s c d -> p s d c"),
+            )
+
+        def quantize_w_enc():
+            nc.vector.quantize_mx(out=w_enc_codes[:].bitcast(E4M3), scales=w_enc_scales[:], in_=w_enc_grouped[:])
+
+        x_grouped = kept("x_grouped", PACK * D_ENC, BF16)
+        x_codes = kept("x_codes", D_ENC, U32)
+        x_scales = kept("x_scales", D_ENC, U8)
+
+        def group_x():
+            nc.scalar.copy(
+                out=x_grouped[:].rearrange("p (c i t) -> p c t i", i=4, t=PACK),
+                in_=x_raw[:].rearrange("p (t c i) -> p c t i", i=4, t=PACK),
+            )
+
+        def quantize_x():
+            nc.vector.quantize_mx(out=x_codes[:].bitcast(E4M3), scales=x_scales[:], in_=x_grouped[:])
+
+
+        def magnitude(i):
+            first, count = STEPS[i]
+            mag = working("magnitude", count * VOCAB, BF16)
+            nc.scalar.activation(out=mag[:], in_=streamed("logits", first, count), func=ACT.Abs, scale=ABS_SCALE)
+            held["mag", i] = mag
+
+        def make_mask(i):
+            first, count = STEPS[i]
+            mask = working("mask", count * VOCAB, BF16)
+            nc.vector.tensor_scalar(
+                out=mask[:], in0=held["mag", i][:], scalar1=ABS_LIMIT, scalar2=None, op0=ALU.is_le
+            )
+            held["mask", i] = mask
+
+        def apply_mask(i):
+            first, count = STEPS[i]
+            dz = working("dz", count * VOCAB, BF16)
+            nc.vector.tensor_tensor(
+                out=dz[:].rearrange("p (h b i) -> p b h i", h=2, i=16),
+                in0=streamed("grad", first, count).rearrange("p (b h i) -> p b h i", h=2, i=16),
+                in1=held["mask", i][:].rearrange("p (b h i) -> p b h i", h=2, i=16),
+                op=ALU.mult,
+            )
+            words = dz[:].bitcast(F32).rearrange("p (h a g q) -> p h a g q", h=2, a=count, g=PASSES)
+            for a in range(count):
+                turned = bank("dz%d" % ((first + a) % 2))
+                for g in range(PASSES):
+                    for h in range(2):
+                        x = 2 * g + h
+                        nc.tensor.transpose(turned[:, x * P : (x + 1) * P], words[:, h, a, g, :], ident_f32[:])
+                held["turned", first + a] = turned
+
+        def group_dz(i, engine):
+            first, count = STEPS[i]
+            if ("grouped", i) not in held:
+                held["grouped", i] = working("dz_grouped", count * VOCAB, BF16)
+            words = held["grouped", i][:].bitcast(F32).rearrange("p (a g r h) -> p a g r h", a=count, g=PASSES, h=2)
+            for a in range(count):
+                owner = "vector" if ((first + a) % 2 == 1 and VEC_FROM <= first + a < VEC_TO) else "scalar"
+                if owner == engine:
+                    src = held["turned", first + a][:].rearrange("p (g h r) -> p g r h", g=PASSES, h=2)
+                    copy_on(engine, words[:, a], src)
+
+        def quantize_dz(i):
+            first, count = STEPS[i]
+            codes = working("dz_codes", count * PASSES * P, U32, bufs=2 + LAG)
+            scales = working("dz_scales", count * PASSES * P, U8, bufs=2 + LAG)
+            nc.vector.quantize_mx(out=codes[:].bitcast(E5M2), scales=scales[:], in_=held["grouped", i][:])
+            held["codes", i] = (codes, scales)
+
+        def multiply(i):
+            first, count = STEPS[i]
+            codes, scales = held["codes", i]
+            for a in range(count):
+                dh = bank("dh%d" % ((first + a) % 4 if first < TILES - 4 else (first + a) % 4 % 3))
+                for g in range(PASSES):
+                    rows = slice((a * PASSES + g) * P, (a * PASSES + g + 1) * P)
+                    cols = slice(g * D_JOINT, (g + 1) * D_JOINT)
+                    nc.tensor.matmul_mx(
+                        out=dh[:],
+                        lhsT=codes[:, rows].bitcast(E5M2),
+                        lhsT_scale=scales[:, rows],
+                        rhs=w_out_codes[:, cols].bitcast(E4M3),
+                        rhs_scale=w_out_scales[:, cols],
+                        start=(g == 0),
+                        stop=(g == PASSES - 1),
+                    )
+                held["dh", first + a] = dh
+
+        def square(i):
+            first, count = STEPS[i]
+            sq = working("square", count * D_JOINT, F32)
+            nc.scalar.activation(
+                out=sq[:].rearrange("p (c b w) -> p b c w", c=PACK, w=8),
+                in_=streamed("joint", first, count).rearrange("p (b c w) -> p b c w", c=PACK, w=8),
+                func=ACT.Square,
+            )
+            held["square", i] = sq
+
+        def through_tanh(i):
+            first, count = STEPS[i]
+            sq = held["square", i][:].rearrange("p (c a q) -> p a c q", c=PACK, a=count)
+            for a in range(count):
+                t, u = divmod(first + a, U)
+                term = working("term", D_JOINT, F32, bufs=4)
+                nc.vector.scalar_tensor_tensor(
+                    out=term[:].rearrange("p (c q) -> p c q", c=PACK),
+                    in0=sq[:, a],
+                    scalar=1.0,
+                    in1=held["dh", first + a][:].rearrange("p (c q) -> p c q", c=PACK),
+                    op0=ALU.subtract,
+                    op1=ALU.mult,
+                )
+                if u == 0:
+                    held["sum", t] = bank("sum%d" % (t % 2))
+                    nc.tensor.matmul(held["sum", t][:], lhsT=zeros[:, :P], rhs=zeros[:], start=True, stop=False)
+                for c in range(PACK):
+                    cols = slice(c * P, (c + 1) * P)
+                    nc.tensor.matmul(
+                        held["sum", t][:, cols],
+                        lhsT=term[:, cols],
+                        rhs=ident_f32[:],
+                        is_transpose=True,
+                        start=False,
+                        stop=(u == U - 1 and c == PACK - 1),
+                    )
+
+        def round_denc(t):
+            denc = kept("denc_%d" % t, D_JOINT, BF16)
+            dst = denc[:].rearrange("p (r c) -> p r c", c=PACK)
+            src = held["sum", t][:].rearrange("p (c r) -> p r c", c=PACK)
+            if t < PACK - 1:
+                nc.scalar.activation(out=dst, in_=src, func=ACT.Copy, scale=-1.0)
+            else:
+                nc.vector.tensor_scalar(out=dst, in0=src, scalar1=-1.0, scalar2=None, op0=ALU.mult)
+            held["denc", t] = denc
+
+        def multiply_out_0(t):
+            codes = working("denc_codes", P, U32)
+            scales = working("denc_scales", P, U8)
+            nc.vector.quantize_mx(out=codes[:].bitcast(E5M2), scales=scales[:], in_=held["denc", t][:])
+            acc = bank("sum%d" % (t % 2))
+            nc.tensor.matmul_mx(
+                out=acc[:],
+                lhsT=codes[:].bitcast(E5M2),
+                lhsT_scale=scales[:],
+                rhs=w_enc_codes[:].bitcast(E4M3),
+                rhs_scale=w_enc_scales[:],
+                start=True,
+                stop=True,
+            )
+            held["out_0", t] = acc
+
+        def empty_out_0(t):
+            rows = kept("out_0_rows_%d" % t, D_ENC, F32)
+            nc.scalar.copy(
+                out=rows[:].rearrange("p (d s) -> p d s", s=PACK),
+                in_=held["out_0", t][:].rearrange("p (s d) -> p d s", s=PACK),
+            )
+            held["rows_0", t] = rows
+
+        def store_out_0(t):
+            nc.sync.dma_start(out=out_0_rows[:, t, :], in_=held["rows_0", t][:])
+
+        def turn_denc(t):
+            words = held["denc", t][:].bitcast(F32)
+            for v in range(2):
+                if t == 0:
+                    held["back", v] = bank(("sum0", "dh3")[v])
+                nc.tensor.transpose(held["back", v][:, t * P : (t + 1) * P], words[:, v : 2 * P : 2], ident_f32[:])
+
+        n = len(STEPS)
+        early = {}
+        late = {}
+
+        def place(where, k, action):
+            where.setdefault(k, []).append(action)
+
+        place(late, W_OUT_AT - 1, sort_w_out)
+        place(early, W_OUT_AT, group_w_out)
+        place(late, W_OUT_AT, quantize_w_out)
+        place(late, W_ENC_AT, sort_w_enc)
+        place(late, W_ENC_AT + 1, lambda: turn_w_enc(0))
+        place(late, W_ENC_AT + 2, lambda: turn_w_enc(1))
+        place(late, W_ENC_AT + 3, quantize_w_enc)
+        place(late, n + 1 + LAG, group_x)
+        for t in range(PACK - 1):
+            place(late, n + 1 + LAG, lambda t=t: turn_denc(t))
+            place(early, n + 1 + LAG, lambda t=t: store_out_0(t))
+        for t in range(PACK - 1):
+            done = STEP_OF[(t + 1) * U - 1] + 3 + LAG
+            place(late, done + 1, lambda t=t: round_denc(t))
+            place(late, done + 2, lambda t=t: multiply_out_0(t))
+            place(late, done + 3, lambda t=t: empty_out_0(t))
+
+        pending = list(LOADS)
+        users = {("joint", "wide"): [W_OUT_AT - 1, W_OUT_AT - 1]}
+
+        def issue_loads(k):
+            while pending:
+                kind, first, count = pending[0]
+                if count:
+                    earlier = users.setdefault((kind, size_of(count)), [])
+                    depth = LOAD_BUFS[size_of(count)]
+                    if len(earlier) >= depth and earlier[-depth] >= k:
+                        break
+                    earlier.append(STEP_OF[first + count - 1] + READER[kind])
+                load(kind, first, count)
+                pending.remove((kind, first, count))
+
+        issue_loads(0)
+        make_identity(nc, ident_f32[:])
+        make_identity(nc, ident_bf16[:])
+        nc.gpsimd.memset(zeros[:], 0.0)
+
+        def stage(action, i, *rest):
+            if 0 <= i < n:
+                action(i, *rest)
+
+        for k in range(n + 3 + LAG):
+            issue_loads(k)
+            stage(group_dz, k - 2, "scalar")
+            stage(make_mask, k - 1)
+            stage(group_dz, k - 2, "vector")
+            for action in early.get(k, []):
+                action()
+            stage(magnitude, k)
+            stage(apply_mask, k - 1)
+            stage(quantize_dz, k - 2)
+            stage(multiply, k - 2 - LAG)
+            stage(square, k - 2 - LAG)
+            stage(through_tanh, k - 3 - LAG)
+            for action in late.get(k, []):
+                action()
+
+        last = PACK - 1
+        round_denc(last)
+        turn_denc(last)
+        multiply_out_0(last)
+        by_frames = working("dz", PACK * D_JOINT, BF16)
+        dst = by_frames[:].rearrange("p (v b e w t) -> p v b e w t", v=2, e=2, w=8, t=PACK)
+        for v in range(2):
+            src = held["back", v][:].bitcast(BF16).rearrange("p (t b w e) -> p b e w t", t=PACK, w=8, e=2)
+            copy_on(("vector", "scalar")[v], dst[:, v], src)
+        quantize_x()
+        codes = kept("denc_frame_codes", D_JOINT, U32)
+        scales = kept("denc_frame_scales", D_JOINT, U8)
+        nc.vector.quantize_mx(out=codes[:].bitcast(E5M2), scales=scales[:], in_=by_frames[:])
+        empty_out_0(last)
+        store_out_0(last)
+        for m in range(D_ENC // P):
+            rows = slice(m * P, (m + 1) * P)
+            acc = bank(("dz0", "dz1", "dh1", "dh2")[m])
+            nc.tensor.matmul_mx(
+                out=acc[:],
+                lhsT=x_codes[:, rows].bitcast(E4M3),
+                lhsT_scale=x_scales[:, rows],
+                rhs=codes[:].bitcast(E5M2),
+                rhs_scale=scales[:],
+                start=True,
+                stop=True,
+            )
+            result = working("term", D_JOINT, F32, bufs=4)
+            copy_on(
+                ("vector", "scalar")[m % 2],
+                result[:].rearrange("p (b v i) -> p b v i", v=2, i=16),
+                acc[:].rearrange("p (v b i) -> p b v i", v=2, i=16),
+            )
+            nc.sync.dma_start(out=out_1[rows, :], in_=result[:])

@@ -39,7 +39,7 @@ STEPS = (
 )
 STEP_OF = {first + a: i for i, (first, count) in enumerate(STEPS) for a in range(count)}
 READER = {"logits": 0, "grad": 1, "joint": 2 + LAG}
-GQ = -0.5
+GQ = 1.2
 JQ = 2.5
 QUEUE = {"logits": 0, "grad": GQ, "joint": JQ + LAG}
 VEC_FROM = 2
@@ -47,18 +47,28 @@ VEC_TO = 28
 WIDE = 4
 LWIDE = 2
 NARROW = 4
+TURN_AT = 1
+FINE = 20
 PIECES = {
     "logits": [s for s in STEPS if s[0] < NARROW] + [(a, LWIDE) for a in range(NARROW, TILES - WIDE, LWIDE)] + [s for s in STEPS if s[0] >= TILES - WIDE],
-    "grad": [(0, 2), (2, 2)] + [(a, WIDE) for a in range(WIDE, TILES - WIDE, WIDE)] + [s for s in STEPS if s[0] >= TILES - WIDE],
-    "joint": [(a, WIDE) for a in range(0, TILES - WIDE, WIDE)] + [s for s in STEPS if s[0] >= TILES - WIDE],
+    "grad": [(0, 2), (2, 2)] + [(a, WIDE) for a in range(WIDE, FINE, WIDE)] + [s for s in STEPS if s[0] >= FINE],
+    "joint": [(0, 2), (2, 2)] + [(a, WIDE) for a in range(WIDE, FINE, WIDE)] + [s for s in STEPS if s[0] >= FINE],
 }
-W_OUT_AT = 1
-W_ENC_AT = 3
+WO0 = 0.2
+WO1 = 0.3
+WE = 1.2
+XQ = 99
+X_AT = 3
+WARM_1 = 0
+WARM_2 = 0
+WARM_3 = 0
+VEC_SKIP = 64
+W_ENC_AT = 2
 LOADS = [
     entry[2:]
     for entry in sorted(
         [(max(0, STEP_OF[first] + QUEUE[kind]), n, kind, first, count) for n, kind in enumerate(PIECES) for first, count in PIECES[kind]]
-        + [(W_OUT_AT - 1, 3, "w_out", 0, 0), (W_ENC_AT, 3, "w_enc", 0, 0), (len(STEPS) + 3 + LAG, 3, "x", 0, 0)]
+        + [(WO0, -1, "w_out", 0, 0), (WO1, -1, "w_out", 1, 0), (WE, -1, "w_enc", 0, 0), (XQ, -1, "x", 0, 0)]
     )
 ]
 LOAD_BUFS = {"wide": 3, "single": 4}
@@ -111,14 +121,14 @@ def tile_jointnetwork_v_kernel(
         def size_of(count):
             return "single" if count == 1 else "wide"
 
-        w_out_raw = landing("joint", "wide", PACK * VOCAB, BF16)
-        w_out_halves = landing("joint", "wide", PACK * VOCAB, BF16)
+        w_out_raw = [kept("w_out_raw_%d" % r, 2 * VOCAB, BF16) for r in range(2)]
         w_enc_raw = kept("w_enc_raw", PACK * D_JOINT, BF16)
         x_raw = kept("x_raw", PACK * D_ENC, BF16)
 
         def load(kind, first, count):
             if kind == "w_out":
-                nc.sync.dma_start(out=w_out_raw[:], in_=W_out.rearrange("(p s) v -> p (s v)", s=PACK))
+                rows = W_out.rearrange("(p r s) v -> p r (s v)", r=2, s=2)
+                nc.sync.dma_start(out=w_out_raw[first][:], in_=rows[:, first, :])
             elif kind == "w_enc":
                 nc.sync.dma_start(out=w_enc_raw[:], in_=W_enc.rearrange("(p s) j -> p (s j)", s=PACK))
             elif kind == "x":
@@ -144,36 +154,29 @@ def tile_jointnetwork_v_kernel(
         w_out_codes = kept("w_out_codes", PASSES * D_JOINT, U32)
         w_out_scales = kept("w_out_scales", PASSES * D_JOINT, U8)
 
-        def sort_w_out():
-            halves = w_out_halves
+        w_out_grouped = kept("w_out_grouped", PASSES * PACK * D_JOINT, BF16)
+
+        def sort_w_out(r):
+            halves = working("dz", 2 * VOCAB, BF16)
             nc.vector.tensor_copy(
                 out=halves[:].bitcast(F32).rearrange("p (h b i) -> p b h i", h=2, i=8),
-                in_=w_out_raw[:].bitcast(F32).rearrange("p (b h i) -> p b h i", h=2, i=8),
+                in_=w_out_raw[r][:].bitcast(F32).rearrange("p (b h i) -> p b h i", h=2, i=8),
             )
-            words = halves[:].bitcast(F32).rearrange("p (h s g q) -> p h s g q", h=2, s=PACK, g=PASSES)
+            words = halves[:].bitcast(F32).rearrange("p (h s g q) -> p h s g q", h=2, s=2, g=PASSES)
             for g in range(PASSES):
-                for r in range(2):
-                    turned = bank("dh%d" % (2 * g + r))
-                    for x in range(4):
-                        s, h = 2 * r + x // 2, x % 2
-                        nc.tensor.transpose(turned[:, x * P : (x + 1) * P], words[:, h, s, g, :], ident_f32[:])
-                    held["w_out", g, r] = turned
+                turned = bank("dh%d" % (2 * r + g))
+                for x in range(4):
+                    nc.tensor.transpose(turned[:, x * P : (x + 1) * P], words[:, x % 2, x // 2, g, :], ident_f32[:])
+                held["w_out", g, r] = turned
 
-        def group_w_out():
+        def group_w_out(r, engine):
+            dst = w_out_grouped[:].bitcast(F32).rearrange("p (g c b w r x) -> p g r b c w x", g=PASSES, c=PACK, w=2, r=2, x=4)
             for g in range(PASSES):
-                grouped = kept("w_out_grouped_%d" % g, PACK * D_JOINT, BF16)
-                held["w_out", g] = grouped
-                dst = grouped[:].bitcast(F32).rearrange("p (c b w r x) -> p r b c w x", c=PACK, w=2, r=2, x=4)
-                for r in range(2):
-                    src = held["w_out", g, r][:].rearrange("p (x b c w) -> p b c w x", x=4, c=PACK, w=2)
-                    copy_on(("scalar", "vector")[g], dst[:, r], src)
+                src = held["w_out", g, r][:].rearrange("p (x b c w) -> p b c w x", x=4, c=PACK, w=2)
+                copy_on(engine, dst[:, g, r], src)
 
         def quantize_w_out():
-            for g in range(PASSES):
-                cols = slice(g * D_JOINT, (g + 1) * D_JOINT)
-                nc.vector.quantize_mx(
-                    out=w_out_codes[:, cols].bitcast(E4M3), scales=w_out_scales[:, cols], in_=held["w_out", g][:]
-                )
+            nc.vector.quantize_mx(out=w_out_codes[:].bitcast(E4M3), scales=w_out_scales[:], in_=w_out_grouped[:])
 
         w_enc_sorted = kept("w_enc_sorted", PACK * D_JOINT, BF16)
         w_enc_grouped = kept("w_enc_grouped", PACK * D_ENC, BF16)
@@ -188,11 +191,15 @@ def tile_jointnetwork_v_kernel(
 
         def turn_w_enc(r):
             rows = w_enc_sorted[:].rearrange("p (c s q) -> p c s q", c=PACK, s=PACK)
-            turned = bank("sum1")
+            turned = bank("sum%d" % (1 - r))
             view = turned[:].bitcast(BF16).rearrange("p (s c d) -> p s c d", s=2, c=PACK)
             for s in range(2):
                 for c in range(PACK):
                     nc.tensor.transpose(view[:, s, c, :], rows[:, c, 2 * r + s, :], ident_bf16[:])
+            held["w_enc", r] = view
+
+        def group_w_enc(r):
+            view = held["w_enc", r]
             half = PACK * D_ENC // 2
             nc.scalar.copy(
                 out=w_enc_grouped[:, r * half : (r + 1) * half].rearrange("p (s d c) -> p s d c", s=2, c=PACK),
@@ -254,7 +261,7 @@ def tile_jointnetwork_v_kernel(
                 held["grouped", i] = working("dz_grouped", count * VOCAB, BF16)
             words = held["grouped", i][:].bitcast(F32).rearrange("p (a g r h) -> p a g r h", a=count, g=PASSES, h=2)
             for a in range(count):
-                owner = "vector" if ((first + a) % 2 == 1 and VEC_FROM <= first + a < VEC_TO) else "scalar"
+                owner = "vector" if ((first + a) % 2 == 1 and VEC_FROM <= first + a < VEC_TO and (first + a) % VEC_SKIP != VEC_SKIP - 1) else "scalar"
                 if owner == engine:
                     src = held["turned", first + a][:].rearrange("p (g h r) -> p g r h", g=PASSES, h=2)
                     copy_on(engine, words[:, a], src)
@@ -284,6 +291,21 @@ def tile_jointnetwork_v_kernel(
                         stop=(g == PASSES - 1),
                     )
                 held["dh", first + a] = dh
+
+        def warm(passes):
+            if passes:
+                codes, scales = held["codes", len(STEPS) - 1]
+                spare = bank("dz0")
+                for g in range(passes):
+                    nc.tensor.matmul_mx(
+                        out=spare[:],
+                        lhsT=codes[:, :P].bitcast(E5M2),
+                        lhsT_scale=scales[:, :P],
+                        rhs=w_out_codes[:, :D_JOINT].bitcast(E4M3),
+                        rhs_scale=w_out_scales[:, :D_JOINT],
+                        start=True,
+                        stop=True,
+                    )
 
         def square(i):
             first, count = STEPS[i]
@@ -327,10 +349,7 @@ def tile_jointnetwork_v_kernel(
             denc = kept("denc_%d" % t, D_JOINT, BF16)
             dst = denc[:].rearrange("p (r c) -> p r c", c=PACK)
             src = held["sum", t][:].rearrange("p (c r) -> p r c", c=PACK)
-            if t < PACK - 1:
-                nc.scalar.activation(out=dst, in_=src, func=ACT.Copy, scale=-1.0)
-            else:
-                nc.vector.tensor_scalar(out=dst, in0=src, scalar1=-1.0, scalar2=None, op0=ALU.mult)
+            nc.scalar.activation(out=dst, in_=src, func=ACT.Copy, scale=-1.0)
             held["denc", t] = denc
 
         def multiply_out_0(t):
@@ -374,17 +393,23 @@ def tile_jointnetwork_v_kernel(
         def place(where, k, action):
             where.setdefault(k, []).append(action)
 
-        place(late, W_OUT_AT - 1, sort_w_out)
-        place(early, W_OUT_AT, group_w_out)
-        place(late, W_OUT_AT, quantize_w_out)
-        place(late, W_ENC_AT, sort_w_enc)
-        place(late, W_ENC_AT + 1, lambda: turn_w_enc(0))
-        place(late, W_ENC_AT + 2, lambda: turn_w_enc(1))
-        place(late, W_ENC_AT + 3, quantize_w_enc)
+        place(late, 0, lambda: sort_w_out(0))
+        place(late, 0, lambda: sort_w_out(1))
+        place(early, 1, lambda: group_w_out(0, "scalar"))
+        place(late, 1, lambda: group_w_out(1, "vector"))
+        place(early, 2, quantize_w_out)
+        place(late, W_ENC_AT - 1, sort_w_enc)
+        place(late, W_ENC_AT - 1, lambda: turn_w_enc(0))
+        place(late, W_ENC_AT - 1, lambda: turn_w_enc(1))
+        place(late, W_ENC_AT, lambda: group_w_enc(1))
+        place(late, W_ENC_AT + 1, lambda: group_w_enc(0))
+        place(late, W_ENC_AT + 2, quantize_w_enc)
         place(late, n + 1 + LAG, group_x)
+        place(late, n + 2 + LAG, quantize_x)
         for t in range(PACK - 1):
-            place(late, n + 1 + LAG, lambda t=t: turn_denc(t))
+            place(late, n + TURN_AT + LAG, lambda t=t: turn_denc(t))
             place(early, n + 1 + LAG, lambda t=t: store_out_0(t))
+        place(late, n + 1 + LAG, lambda: warm(WARM_1))
         for t in range(PACK - 1):
             done = STEP_OF[(t + 1) * U - 1] + 3 + LAG
             place(late, done + 1, lambda t=t: round_denc(t))
@@ -392,7 +417,7 @@ def tile_jointnetwork_v_kernel(
             place(late, done + 3, lambda t=t: empty_out_0(t))
 
         pending = list(LOADS)
-        users = {("joint", "wide"): [W_OUT_AT - 1, W_OUT_AT - 1]}
+        users = {}
 
         def issue_loads(k):
             while pending:
@@ -432,6 +457,7 @@ def tile_jointnetwork_v_kernel(
                 action()
 
         last = PACK - 1
+        warm(WARM_2)
         round_denc(last)
         turn_denc(last)
         multiply_out_0(last)
@@ -440,7 +466,7 @@ def tile_jointnetwork_v_kernel(
         for v in range(2):
             src = held["back", v][:].bitcast(BF16).rearrange("p (t b w e) -> p b e w t", t=PACK, w=8, e=2)
             copy_on(("vector", "scalar")[v], dst[:, v], src)
-        quantize_x()
+        warm(WARM_3)
         codes = kept("denc_frame_codes", D_JOINT, U32)
         scales = kept("denc_frame_scales", D_JOINT, U8)
         nc.vector.quantize_mx(out=codes[:].bitcast(E5M2), scales=scales[:], in_=by_frames[:])

@@ -30,7 +30,7 @@ ABS_SCALE = 19.0
 ABS_LIMIT = 15.0 * ABS_SCALE
 
 HEAD_SINGLES = 2
-TAIL_SINGLES = 4
+TAIL_SINGLES = 8
 LAG = 0
 STEPS = (
     [(a, 1) for a in range(HEAD_SINGLES)]
@@ -44,16 +44,25 @@ JQ = 2.5
 QUEUE = {"logits": 0, "grad": GQ, "joint": JQ + LAG}
 VEC_FROM = 2
 VEC_TO = 28
-WIDE = 4
-LWIDE = 2
-NARROW = 4
+LWIDE = 4
 TURN_AT = 1
-FINE = 20
-PIECES = {
-    "logits": [s for s in STEPS if s[0] < NARROW] + [(a, LWIDE) for a in range(NARROW, TILES - WIDE, LWIDE)] + [s for s in STEPS if s[0] >= TILES - WIDE],
-    "grad": [(0, 2), (2, 2)] + [(a, WIDE) for a in range(WIDE, FINE, WIDE)] + [s for s in STEPS if s[0] >= FINE],
-    "joint": [(0, 2), (2, 2)] + [(a, WIDE) for a in range(WIDE, FINE, WIDE)] + [s for s in STEPS if s[0] >= FINE],
-}
+L_HEAD = [1, 1, 2]
+L_TAIL = [2, 2, 2, 1, 1]
+G_HEAD = [4]
+G_TAIL = [4]
+J_HEAD = [4]
+J_TAIL = [2, 1, 1]
+GWIDE = 4
+JWIDE = 4
+
+
+def cut(head, wide, tail):
+    sizes = head + [wide] * ((TILES - sum(head) - sum(tail)) // wide) + tail
+    assert sum(sizes) == TILES
+    return [(sum(sizes[:n]), size) for n, size in enumerate(sizes)]
+
+
+PIECES = {"logits": cut(L_HEAD, LWIDE, L_TAIL), "grad": cut(G_HEAD, GWIDE, G_TAIL), "joint": cut(J_HEAD, JWIDE, J_TAIL)}
 WO0 = 0.2
 WO1 = 0.3
 WE = 1.2
@@ -71,7 +80,8 @@ LOADS = [
         + [(WO0, -1, "w_out", 0, 0), (WO1, -1, "w_out", 1, 0), (WE, -1, "w_enc", 0, 0), (XQ, -1, "x", 0, 0)]
     )
 ]
-LOAD_BUFS = {"wide": 3, "single": 4}
+WB = 3
+LOAD_BUFS = {"wide": WB, "single": 2}
 
 
 def tile_jointnetwork_v_kernel(
@@ -100,10 +110,10 @@ def tile_jointnetwork_v_kernel(
             return psum.tile([P, BANK], F32, name="bank_" + role, tag=role)
 
         def kept(name, width, dtype):
-            return keep.tile([P, width], dtype, name=name, tag=name, align_bytes=64)
+            return keep.tile([P, width], dtype, name=name, tag=name, align_bytes=256)
 
         def working(name, width, dtype, bufs=2):
-            return work.tile([P, width], dtype, name=name, tag=name, bufs=bufs, align_bytes=64)
+            return work.tile([P, width], dtype, name=name, tag=name, bufs=bufs, align_bytes=256)
 
         def copy_on(engine, out, in_):
             if engine == "scalar":
@@ -116,7 +126,7 @@ def tile_jointnetwork_v_kernel(
 
         def landing(kind, size, width, dtype):
             name = kind + "_" + size
-            return stream.tile([P, width], dtype, name=name, tag=name, bufs=LOAD_BUFS[size], align_bytes=64)
+            return stream.tile([P, width], dtype, name=name, tag=name, bufs=LOAD_BUFS[size], align_bytes=256)
 
         def size_of(count):
             return "single" if count == 1 else "wide"
@@ -214,9 +224,9 @@ def tile_jointnetwork_v_kernel(
         x_scales = kept("x_scales", D_ENC, U8)
 
         def group_x():
-            nc.scalar.copy(
-                out=x_grouped[:].rearrange("p (c i t) -> p c t i", i=4, t=PACK),
-                in_=x_raw[:].rearrange("p (t c i) -> p c t i", i=4, t=PACK),
+            nc.vector.tensor_copy(
+                out=x_grouped[:].rearrange("p (d t) -> p d t", t=PACK),
+                in_=x_raw[:].rearrange("p (t d) -> p d t", t=PACK),
             )
 
         def quantize_x():
@@ -311,8 +321,8 @@ def tile_jointnetwork_v_kernel(
             first, count = STEPS[i]
             sq = working("square", count * D_JOINT, F32)
             nc.scalar.activation(
-                out=sq[:].rearrange("p (c b w) -> p b c w", c=PACK, w=8),
-                in_=streamed("joint", first, count).rearrange("p (b c w) -> p b c w", c=PACK, w=8),
+                out=sq[:].rearrange("p (c b w) -> p c b w", c=PACK, w=8),
+                in_=streamed("joint", first, count).rearrange("p (b c w) -> p c b w", c=PACK, w=8),
                 func=ACT.Square,
             )
             held["square", i] = sq
@@ -404,8 +414,7 @@ def tile_jointnetwork_v_kernel(
         place(late, W_ENC_AT, lambda: group_w_enc(1))
         place(late, W_ENC_AT + 1, lambda: group_w_enc(0))
         place(late, W_ENC_AT + 2, quantize_w_enc)
-        place(late, n + 1 + LAG, group_x)
-        place(late, n + 2 + LAG, quantize_x)
+        place(late, n + 2 + LAG, group_x)
         for t in range(PACK - 1):
             place(late, n + TURN_AT + LAG, lambda t=t: turn_denc(t))
             place(early, n + 1 + LAG, lambda t=t: store_out_0(t))
@@ -461,6 +470,7 @@ def tile_jointnetwork_v_kernel(
         round_denc(last)
         turn_denc(last)
         multiply_out_0(last)
+        quantize_x()
         by_frames = working("dz", PACK * D_JOINT, BF16)
         dst = by_frames[:].rearrange("p (v b e w t) -> p v b e w t", v=2, e=2, w=8, t=PACK)
         for v in range(2):

@@ -44,16 +44,16 @@ JQ = 2.5
 QUEUE = {"logits": 0, "grad": GQ, "joint": JQ + LAG}
 VEC_FROM = 2
 VEC_TO = 28
-LWIDE = 4
+LWIDE = 2
 TURN_AT = 1
 L_HEAD = [1, 1, 2]
-L_TAIL = [2, 2, 2, 1, 1]
-G_HEAD = [4]
-G_TAIL = [4]
-J_HEAD = [4]
+L_TAIL = [1, 1]
+G_HEAD = [2]
+G_TAIL = [2]
+J_HEAD = [2]
 J_TAIL = [2, 1, 1]
-GWIDE = 4
-JWIDE = 4
+GWIDE = 2
+JWIDE = 2
 
 
 def cut(head, wide, tail):
@@ -80,8 +80,16 @@ LOADS = [
         + [(WO0, -1, "w_out", 0, 0), (WO1, -1, "w_out", 1, 0), (WE, -1, "w_enc", 0, 0), (XQ, -1, "x", 0, 0)]
     )
 ]
-WB = 3
-LOAD_BUFS = {"wide": WB, "single": 2}
+WB = 2
+LEAD = 1
+JLEAD = 1
+KINDS = ("grad", "joint")
+SECOND_TO = 24
+SECOND_FROM = 4
+SECOND = [ld for ld in LOADS if ld[0] in KINDS and SECOND_FROM <= ld[1] < SECOND_TO]
+GB = 4
+JB = 4
+LOAD_BUFS = {"logits_wide": WB, "grad_wide": GB, "joint_wide": JB, "logits_single": 2, "grad_single": 2, "joint_single": 2}
 
 
 def tile_jointnetwork_v_kernel(
@@ -126,7 +134,7 @@ def tile_jointnetwork_v_kernel(
 
         def landing(kind, size, width, dtype):
             name = kind + "_" + size
-            return stream.tile([P, width], dtype, name=name, tag=name, bufs=LOAD_BUFS[size], align_bytes=256)
+            return stream.tile([P, width], dtype, name=name, tag=name, bufs=LOAD_BUFS[name], align_bytes=256)
 
         def size_of(count):
             return "single" if count == 1 else "wide"
@@ -148,7 +156,8 @@ def tile_jointnetwork_v_kernel(
                 source, width, dtype = streams[kind]
                 dst = landing(kind, size_of(count), count * width, dtype)
                 t, u = divmod(first, U)
-                nc.sync.dma_start(out=dst[:], in_=source[:, t, u * width : (u + count) * width])
+                queue = nc.scalar if (kind, first, count) in SECOND else nc.sync
+                queue.dma_start(out=dst[:], in_=source[:, t, u * width : (u + count) * width])
                 for a in range(count):
                     loaded[kind, first + a] = (dst, a)
 
@@ -425,22 +434,26 @@ def tile_jointnetwork_v_kernel(
             place(late, done + 2, lambda t=t: multiply_out_0(t))
             place(late, done + 3, lambda t=t: empty_out_0(t))
 
-        pending = list(LOADS)
+        pending = [ld for ld in LOADS if ld not in SECOND]
         users = {}
 
         def issue_loads(k):
+            for kind, first, count in SECOND:
+                if STEP_OF[first] + READER[kind] - (LEAD if kind == "grad" else JLEAD) == k:
+                    users.setdefault((kind, size_of(count)), []).append(STEP_OF[first + count - 1] + READER[kind])
+                    load(kind, first, count)
             while pending:
                 kind, first, count = pending[0]
                 if count:
                     earlier = users.setdefault((kind, size_of(count)), [])
-                    depth = LOAD_BUFS[size_of(count)]
+                    depth = LOAD_BUFS[kind + "_" + size_of(count)]
                     if len(earlier) >= depth and earlier[-depth] >= k:
                         break
                     earlier.append(STEP_OF[first + count - 1] + READER[kind])
                 load(kind, first, count)
                 pending.remove((kind, first, count))
 
-        issue_loads(0)
+        issue_loads(-1)
         make_identity(nc, ident_f32[:])
         make_identity(nc, ident_bf16[:])
         nc.gpsimd.memset(zeros[:], 0.0)
@@ -500,4 +513,4 @@ def tile_jointnetwork_v_kernel(
                 result[:].rearrange("p (b v i) -> p b v i", v=2, i=16),
                 acc[:].rearrange("p (v b i) -> p b v i", v=2, i=16),
             )
-            nc.sync.dma_start(out=out_1[rows, :], in_=result[:])
+            (nc.sync, nc.scalar)[m % 2].dma_start(out=out_1[rows, :], in_=result[:])

from contextlib import ExitStack

import concourse.mybir as mybir
from concourse.masks import make_identity

B, T, U, D_ENC, D_JOINT, VOCAB = 4, 128, 8, 512, 512, 1024
FRAMES = B * T
FLOPS = 2 * FRAMES * U * VOCAB * D_JOINT + 2 * 2 * FRAMES * D_JOINT * D_ENC
BYTES = (
    FRAMES * U * (VOCAB * 4 + VOCAB * 2 + D_JOINT * 4)
    + 2 * (FRAMES * D_ENC + D_ENC * D_JOINT + D_JOINT * VOCAB)
    + 4 * (FRAMES * D_ENC + D_ENC * D_JOINT)
)

F32 = mybir.dt.float32
BF16 = mybir.dt.bfloat16
U32 = mybir.dt.uint32
U8 = mybir.dt.uint8
E4M3 = mybir.dt.float8_e4m3fn_x4
E5M2 = mybir.dt.float8_e5m2_x4
ACT = mybir.ActivationFunctionType
ALU = mybir.AluOpType

P = 128
PACK = 4
BANK = 512
TILES = PACK * U
PASSES = VOCAB // (P * PACK)
ABS_SCALE = 19.0
ABS_LIMIT = 15.0 * ABS_SCALE

HEAD_SINGLES = 2
TAIL_SINGLES = 8
LAG = 0
STEPS = (
    [(a, 1) for a in range(HEAD_SINGLES)]
    + [(a, 2) for a in range(HEAD_SINGLES, TILES - TAIL_SINGLES, 2)]
    + [(a, 1) for a in range(TILES - TAIL_SINGLES, TILES)]
)
STEP_OF = {first + a: i for i, (first, count) in enumerate(STEPS) for a in range(count)}
READER = {"logits": 0, "grad": 1, "joint": 2 + LAG}
GQ = 1.2
JQ = 2.5
QUEUE = {"logits": 0, "grad": GQ, "joint": JQ + LAG}
VEC_FROM = 2
VEC_TO = 28
LWIDE = 2
TURN_AT = 1
L_HEAD = [1, 1, 2]
L_TAIL = [1, 1]
G_HEAD = [2]
G_TAIL = [2]
J_HEAD = [2]
J_TAIL = [2, 1, 1]
GWIDE = 2
JWIDE = 2


def cut(head, wide, tail):
    sizes = head + [wide] * ((TILES - sum(head) - sum(tail)) // wide) + tail
    assert sum(sizes) == TILES
    return [(sum(sizes[:n]), size) for n, size in enumerate(sizes)]


PIECES = {"logits": cut(L_HEAD, LWIDE, L_TAIL), "grad": cut(G_HEAD, GWIDE, G_TAIL), "joint": cut(J_HEAD, JWIDE, J_TAIL)}
WO0 = 0.2
WO1 = 0.3
WE = 1.2
XQ = 99
X_AT = 3
WARM_1 = 0
WARM_2 = 0
WARM_3 = 0
VEC_SKIP = 64
W_ENC_AT = 2
LOADS = [
    entry[2:]
    for entry in sorted(
        [(max(0, STEP_OF[first] + QUEUE[kind]), n, kind, first, count) for n, kind in enumerate(PIECES) for first, count in PIECES[kind]]
        + [(WO0, -1, "w_out", 0, 0), (WO1, -1, "w_out", 1, 0), (WE, -1, "w_enc", 0, 0), (XQ, -1, "x", 0, 0)]
    )
]
WB = 2
LEAD = 1
JLEAD = 1
KINDS = ("grad", "joint")
SECOND_TO = 24
SECOND_FROM = 4
SECOND = [ld for ld in LOADS if ld[0] in KINDS and SECOND_FROM <= ld[1] < SECOND_TO]
GB = 4
JB = 4
LOAD_BUFS = {"logits_wide": WB, "grad_wide": GB, "joint_wide": JB, "logits_single": 2, "grad_single": 2, "joint_single": 2}


def tile_jointnetwork_v_kernel(
    tc, encoder_out, predictor_out, W_enc, b_enc, W_pred, b_pred, W_out, b_out, joint, logits, grad_out, out_0, out_1
):
    nc = tc.nc

    def by_frame(x):
        return x.rearrange("b f u w -> (b f) (u w)").rearrange("(p t) w -> p t w", t=PACK)

    streams = {
        "logits": (by_frame(logits), VOCAB, F32),
        "grad": (by_frame(grad_out), VOCAB, BF16),
        "joint": (by_frame(joint), D_JOINT, F32),
    }
    out_0_rows = out_0.rearrange("b f d -> (b f) d").rearrange("(p t) d -> p t d", t=PACK)

    with ExitStack() as ctx:
        keep = ctx.enter_context(tc.tile_pool(name="keep", bufs=1))
        stream = ctx.enter_context(tc.tile_pool(name="stream", bufs=1))
        work = ctx.enter_context(tc.tile_pool(name="work", bufs=2))
        psum = ctx.enter_context(tc.psum_pool(name="psum", bufs=1))
        ctx.enter_context(tc.manual_schedule())

        def bank(role):
            return psum.tile([P, BANK], F32, name="bank_" + role, tag=role)

        def kept(name, width, dtype):
            return keep.tile([P, width], dtype, name=name, tag=name, align_bytes=256)

        def working(name, width, dtype, bufs=2):
            return work.tile([P, width], dtype, name=name, tag=name, bufs=bufs, align_bytes=256)

        def copy_on(engine, out, in_):
            if engine == "scalar":
                nc.scalar.copy(out=out, in_=in_)
            else:
                nc.vector.tensor_copy(out=out, in_=in_)

        loaded = {}
        held = {}

        def landing(kind, size, width, dtype):
            name = kind + "_" + size
            return stream.tile([P, width], dtype, name=name, tag=name, bufs=LOAD_BUFS[name], align_bytes=256)

        def size_of(count):
            return "single" if count == 1 else "wide"

        w_out_raw = [kept("w_out_raw_%d" % r, 2 * VOCAB, BF16) for r in range(2)]
        w_enc_raw = kept("w_enc_raw", PACK * D_JOINT, BF16)
        x_raw = kept("x_raw", PACK * D_ENC, BF16)

        def load(kind, first, count):
            if kind == "w_out":
                rows = W_out.rearrange("(p r s) v -> p r (s v)", r=2, s=2)
                nc.sync.dma_start(out=w_out_raw[first][:], in_=rows[:, first, :])
            elif kind == "w_enc":
                nc.sync.dma_start(out=w_enc_raw[:], in_=W_enc.rearrange("(p s) j -> p (s j)", s=PACK))
            elif kind == "x":
                rows = encoder_out.rearrange("b f d -> (b f) d")
                nc.sync.dma_start(out=x_raw[:], in_=rows.rearrange("(p t) d -> p (t d)", t=PACK))
            else:
                source, width, dtype = streams[kind]
                dst = landing(kind, size_of(count), count * width, dtype)
                t, u = divmod(first, U)
                queue = nc.scalar if (kind, first, count) in SECOND else nc.sync
                queue.dma_start(out=dst[:], in_=source[:, t, u * width : (u + count) * width])
                for a in range(count):
                    loaded[kind, first + a] = (dst, a)

        def streamed(kind, first, count):
            dst, a = loaded[kind, first]
            width = streams[kind][1]
            return dst[:, a * width : (a + count) * width]

        ident_f32 = kept("ident_f32", P, F32)
        ident_bf16 = kept("ident_bf16", P, BF16)
        zeros = kept("zeros", BANK, BF16)

        w_out_codes = kept("w_out_codes", PASSES * D_JOINT, U32)
        w_out_scales = kept("w_out_scales", PASSES * D_JOINT, U8)

        w_out_grouped = kept("w_out_grouped", PASSES * PACK * D_JOINT, BF16)

        def sort_w_out(r):
            halves = working("dz", 2 * VOCAB, BF16)
            nc.vector.tensor_copy(
                out=halves[:].bitcast(F32).rearrange("p (h b i) -> p b h i", h=2, i=8),
                in_=w_out_raw[r][:].bitcast(F32).rearrange("p (b h i) -> p b h i", h=2, i=8),
            )
            words = halves[:].bitcast(F32).rearrange("p (h s g q) -> p h s g q", h=2, s=2, g=PASSES)
            for g in range(PASSES):
                turned = bank("dh%d" % (2 * r + g))
                for x in range(4):
                    nc.tensor.transpose(turned[:, x * P : (x + 1) * P], words[:, x % 2, x // 2, g, :], ident_f32[:])
                held["w_out", g, r] = turned

        def group_w_out(r, engine):
            dst = w_out_grouped[:].bitcast(F32).rearrange("p (g c b w r x) -> p g r b c w x", g=PASSES, c=PACK, w=2, r=2, x=4)
            for g in range(PASSES):
                src = held["w_out", g, r][:].rearrange("p (x b c w) -> p b c w x", x=4, c=PACK, w=2)
                copy_on(engine, dst[:, g, r], src)

        def quantize_w_out():
            nc.vector.quantize_mx(out=w_out_codes[:].bitcast(E4M3), scales=w_out_scales[:], in_=w_out_grouped[:])

        w_enc_sorted = kept("w_enc_sorted", PACK * D_JOINT, BF16)
        w_enc_grouped = kept("w_enc_grouped", PACK * D_ENC, BF16)
        w_enc_codes = kept("w_enc_codes", D_ENC, U32)
        w_enc_scales = kept("w_enc_scales", D_ENC, U8)

        def sort_w_enc():
            nc.vector.tensor_copy(
                out=w_enc_sorted[:].bitcast(F32).rearrange("p (c b i) -> p b c i", c=PACK, i=4),
                in_=w_enc_raw[:].bitcast(F32).rearrange("p (b c i) -> p b c i", c=PACK, i=4),
            )

        def turn_w_enc(r):
            rows = w_enc_sorted[:].rearrange("p (c s q) -> p c s q", c=PACK, s=PACK)
            turned = bank("sum%d" % (1 - r))
            view = turned[:].bitcast(BF16).rearrange("p (s c d) -> p s c d", s=2, c=PACK)
            for s in range(2):
                for c in range(PACK):
                    nc.tensor.transpose(view[:, s, c, :], rows[:, c, 2 * r + s, :], ident_bf16[:])
            held["w_enc", r] = view

        def group_w_enc(r):
            view = held["w_enc", r]
            half = PACK * D_ENC // 2
            nc.scalar.copy(
                out=w_enc_grouped[:, r * half : (r + 1) * half].rearrange("p (s d c) -> p s d c", s=2, c=PACK),
                in_=view.rearrange("p s c d -> p s d c"),
            )

        def quantize_w_enc():
            nc.vector.quantize_mx(out=w_enc_codes[:].bitcast(E4M3), scales=w_enc_scales[:], in_=w_enc_grouped[:])

        x_grouped = kept("x_grouped", PACK * D_ENC, BF16)
        x_codes = kept("x_codes", D_ENC, U32)
        x_scales = kept("x_scales", D_ENC, U8)

        def group_x():
            nc.vector.tensor_copy(
                out=x_grouped[:].rearrange("p (d t) -> p d t", t=PACK),
                in_=x_raw[:].rearrange("p (t d) -> p d t", t=PACK),
            )

        def quantize_x():
            nc.vector.quantize_mx(out=x_codes[:].bitcast(E4M3), scales=x_scales[:], in_=x_grouped[:])


        def magnitude(i):
            first, count = STEPS[i]
            mag = working("magnitude", count * VOCAB, BF16)
            nc.scalar.activation(out=mag[:], in_=streamed("logits", first, count), func=ACT.Abs, scale=ABS_SCALE)
            held["mag", i] = mag

        def make_mask(i):
            first, count = STEPS[i]
            mask = working("mask", count * VOCAB, BF16)
            nc.vector.tensor_scalar(
                out=mask[:], in0=held["mag", i][:], scalar1=ABS_LIMIT, scalar2=None, op0=ALU.is_le
            )
            held["mask", i] = mask

        def apply_mask(i):
            first, count = STEPS[i]
            dz = working("dz", count * VOCAB, BF16)
            nc.vector.tensor_tensor(
                out=dz[:].rearrange("p (h b i) -> p b h i", h=2, i=16),
                in0=streamed("grad", first, count).rearrange("p (b h i) -> p b h i", h=2, i=16),
                in1=held["mask", i][:].rearrange("p (b h i) -> p b h i", h=2, i=16),
                op=ALU.mult,
            )
            words = dz[:].bitcast(F32).rearrange("p (h a g q) -> p h a g q", h=2, a=count, g=PASSES)
            for a in range(count):
                turned = bank("dz%d" % ((first + a) % 2))
                for g in range(PASSES):
                    for h in range(2):
                        x = 2 * g + h
                        nc.tensor.transpose(turned[:, x * P : (x + 1) * P], words[:, h, a, g, :], ident_f32[:])
                held["turned", first + a] = turned

        def group_dz(i, engine):
            first, count = STEPS[i]
            if ("grouped", i) not in held:
                held["grouped", i] = working("dz_grouped", count * VOCAB, BF16)
            words = held["grouped", i][:].bitcast(F32).rearrange("p (a g r h) -> p a g r h", a=count, g=PASSES, h=2)
            for a in range(count):
                owner = "vector" if ((first + a) % 2 == 1 and VEC_FROM <= first + a < VEC_TO and (first + a) % VEC_SKIP != VEC_SKIP - 1) else "scalar"
                if owner == engine:
                    src = held["turned", first + a][:].rearrange("p (g h r) -> p g r h", g=PASSES, h=2)
                    copy_on(engine, words[:, a], src)

        def quantize_dz(i):
            first, count = STEPS[i]
            codes = working("dz_codes", count * PASSES * P, U32, bufs=2 + LAG)
            scales = working("dz_scales", count * PASSES * P, U8, bufs=2 + LAG)
            nc.vector.quantize_mx(out=codes[:].bitcast(E5M2), scales=scales[:], in_=held["grouped", i][:])
            held["codes", i] = (codes, scales)

        def multiply(i):
            first, count = STEPS[i]
            codes, scales = held["codes", i]
            for a in range(count):
                dh = bank("dh%d" % ((first + a) % 4 if first < TILES - 4 else (first + a) % 4 % 3))
                for g in range(PASSES):
                    rows = slice((a * PASSES + g) * P, (a * PASSES + g + 1) * P)
                    cols = slice(g * D_JOINT, (g + 1) * D_JOINT)
                    nc.tensor.matmul_mx(
                        out=dh[:],
                        lhsT=codes[:, rows].bitcast(E5M2),
                        lhsT_scale=scales[:, rows],
                        rhs=w_out_codes[:, cols].bitcast(E4M3),
                        rhs_scale=w_out_scales[:, cols],
                        start=(g == 0),
                        stop=(g == PASSES - 1),
                    )
                held["dh", first + a] = dh

        def warm(passes):
            if passes:
                codes, scales = held["codes", len(STEPS) - 1]
                spare = bank("dz0")
                for g in range(passes):
                    nc.tensor.matmul_mx(
                        out=spare[:],
                        lhsT=codes[:, :P].bitcast(E5M2),
                        lhsT_scale=scales[:, :P],
                        rhs=w_out_codes[:, :D_JOINT].bitcast(E4M3),
                        rhs_scale=w_out_scales[:, :D_JOINT],
                        start=True,
                        stop=True,
                    )

        def square(i):
            first, count = STEPS[i]
            sq = working("square", count * D_JOINT, F32)
            nc.scalar.activation(
                out=sq[:].rearrange("p (c b w) -> p c b w", c=PACK, w=8),
                in_=streamed("joint", first, count).rearrange("p (b c w) -> p c b w", c=PACK, w=8),
                func=ACT.Square,
            )
            held["square", i] = sq

        def through_tanh(i):
            first, count = STEPS[i]
            sq = held["square", i][:].rearrange("p (c a q) -> p a c q", c=PACK, a=count)
            for a in range(count):
                t, u = divmod(first + a, U)
                term = working("term", D_JOINT, F32, bufs=4)
                nc.vector.scalar_tensor_tensor(
                    out=term[:].rearrange("p (c q) -> p c q", c=PACK),
                    in0=sq[:, a],
                    scalar=1.0,
                    in1=held["dh", first + a][:].rearrange("p (c q) -> p c q", c=PACK),
                    op0=ALU.subtract,
                    op1=ALU.mult,
                )
                if u == 0:
                    held["sum", t] = bank("sum%d" % (t % 2))
                    nc.tensor.matmul(held["sum", t][:], lhsT=zeros[:, :P], rhs=zeros[:], start=True, stop=False)
                for c in range(PACK):
                    cols = slice(c * P, (c + 1) * P)
                    nc.tensor.matmul(
                        held["sum", t][:, cols],
                        lhsT=term[:, cols],
                        rhs=ident_f32[:],
                        is_transpose=True,
                        start=False,
                        stop=(u == U - 1 and c == PACK - 1),
                    )

        def round_denc(t):
            denc = kept("denc_%d" % t, D_JOINT, BF16)
            dst = denc[:].rearrange("p (r c) -> p r c", c=PACK)
            src = held["sum", t][:].rearrange("p (c r) -> p r c", c=PACK)
            nc.scalar.activation(out=dst, in_=src, func=ACT.Copy, scale=-1.0)
            held["denc", t] = denc

        def multiply_out_0(t):
            codes = working("denc_codes", P, U32)
            scales = working("denc_scales", P, U8)
            nc.vector.quantize_mx(out=codes[:].bitcast(E5M2), scales=scales[:], in_=held["denc", t][:])
            acc = bank("sum%d" % (t % 2))
            nc.tensor.matmul_mx(
                out=acc[:],
                lhsT=codes[:].bitcast(E5M2),
                lhsT_scale=scales[:],
                rhs=w_enc_codes[:].bitcast(E4M3),
                rhs_scale=w_enc_scales[:],
                start=True,
                stop=True,
            )
            held["out_0", t] = acc

        def empty_out_0(t):
            rows = kept("out_0_rows_%d" % t, D_ENC, F32)
            nc.scalar.copy(
                out=rows[:].rearrange("p (d s) -> p d s", s=PACK),
                in_=held["out_0", t][:].rearrange("p (s d) -> p d s", s=PACK),
            )
            held["rows_0", t] = rows

        def store_out_0(t):
            nc.sync.dma_start(out=out_0_rows[:, t, :], in_=held["rows_0", t][:])

        def turn_denc(t):
            words = held["denc", t][:].bitcast(F32)
            for v in range(2):
                if t == 0:
                    held["back", v] = bank(("sum0", "dh3")[v])
                nc.tensor.transpose(held["back", v][:, t * P : (t + 1) * P], words[:, v : 2 * P : 2], ident_f32[:])

        n = len(STEPS)
        early = {}
        late = {}

        def place(where, k, action):
            where.setdefault(k, []).append(action)

        place(late, 0, lambda: sort_w_out(0))
        place(late, 0, lambda: sort_w_out(1))
        place(early, 1, lambda: group_w_out(0, "scalar"))
        place(late, 1, lambda: group_w_out(1, "vector"))
        place(early, 2, quantize_w_out)
        place(late, W_ENC_AT - 1, sort_w_enc)
        place(late, W_ENC_AT - 1, lambda: turn_w_enc(0))
        place(late, W_ENC_AT - 1, lambda: turn_w_enc(1))
        place(late, W_ENC_AT, lambda: group_w_enc(1))
        place(late, W_ENC_AT + 1, lambda: group_w_enc(0))
        place(late, W_ENC_AT + 2, quantize_w_enc)
        place(late, n + 2 + LAG, group_x)
        for t in range(PACK - 1):
            place(late, n + TURN_AT + LAG, lambda t=t: turn_denc(t))
            place(early, n + 1 + LAG, lambda t=t: store_out_0(t))
        place(late, n + 1 + LAG, lambda: warm(WARM_1))
        for t in range(PACK - 1):
            done = STEP_OF[(t + 1) * U - 1] + 3 + LAG
            place(late, done + 1, lambda t=t: round_denc(t))
            place(late, done + 2, lambda t=t: multiply_out_0(t))
            place(late, done + 3, lambda t=t: empty_out_0(t))

        pending = [ld for ld in LOADS if ld not in SECOND]
        users = {}

        def issue_loads(k):
            for kind, first, count in SECOND:
                if STEP_OF[first] + READER[kind] - (LEAD if kind == "grad" else JLEAD) == k:
                    users.setdefault((kind, size_of(count)), []).append(STEP_OF[first + count - 1] + READER[kind])
                    load(kind, first, count)
            while pending:
                kind, first, count = pending[0]
                if count:
                    earlier = users.setdefault((kind, size_of(count)), [])
                    depth = LOAD_BUFS[kind + "_" + size_of(count)]
                    if len(earlier) >= depth and earlier[-depth] >= k:
                        break
                    earlier.append(STEP_OF[first + count - 1] + READER[kind])
                load(kind, first, count)
                pending.remove((kind, first, count))

        issue_loads(-1)
        make_identity(nc, ident_f32[:])
        make_identity(nc, ident_bf16[:])
        nc.gpsimd.memset(zeros[:], 0.0)

        def stage(action, i, *rest):
            if 0 <= i < n:
                action(i, *rest)

        for k in range(n + 3 + LAG):
            issue_loads(k)
            stage(group_dz, k - 2, "scalar")
            stage(make_mask, k - 1)
            stage(group_dz, k - 2, "vector")
            for action in early.get(k, []):
                action()
            stage(magnitude, k)
            stage(apply_mask, k - 1)
            stage(quantize_dz, k - 2)
            stage(multiply, k - 2 - LAG)
            stage(square, k - 2 - LAG)
            stage(through_tanh, k - 3 - LAG)
            for action in late.get(k, []):
                action()

        last = PACK - 1
        warm(WARM_2)
        round_denc(last)
        turn_denc(last)
        multiply_out_0(last)
        quantize_x()
        by_frames = working("dz", PACK * D_JOINT, BF16)
        dst = by_frames[:].rearrange("p (v b e w t) -> p v b e w t", v=2, e=2, w=8, t=PACK)
        for v in range(2):
            src = held["back", v][:].bitcast(BF16).rearrange("p (t b w e) -> p b e w t", t=PACK, w=8, e=2)
            copy_on(("vector", "scalar")[v], dst[:, v], src)
        warm(WARM_3)
        codes = kept("denc_frame_codes", D_JOINT, U32)
        scales = kept("denc_frame_scales", D_JOINT, U8)
        nc.vector.quantize_mx(out=codes[:].bitcast(E5M2), scales=scales[:], in_=by_frames[:])
        empty_out_0(last)
        store_out_0(last)
        for m in range(D_ENC // P):
            rows = slice(m * P, (m + 1) * P)
            acc = bank(("dz0", "dz1", "dh1", "dh2")[m])
            nc.tensor.matmul_mx(
                out=acc[:],
                lhsT=x_codes[:, rows].bitcast(E4M3),
                lhsT_scale=x_scales[:, rows],
                rhs=codes[:].bitcast(E5M2),
                rhs_scale=scales[:],
                start=True,
                stop=True,
            )
            result = working("term", D_JOINT, F32, bufs=4)
            copy_on(
                ("vector", "scalar")[m % 2],
                result[:].rearrange("p (b v i) -> p b v i", v=2, i=16),
                acc[:].rearrange("p (v b i) -> p b v i", v=2, i=16),
            )
            (nc.sync, nc.scalar)[m % 2].dma_start(out=out_1[rows, :], in_=result[:])
